import numpy as np
import ml_dtypes


def mxq(x, axis, fmt="e4m3"):
    dtype, down = {"e4m3": (ml_dtypes.float8_e4m3fn, 7), "e5m2": (ml_dtypes.float8_e5m2, 14)}[fmt]
    v = np.moveaxis(np.asarray(x, np.float32).astype(ml_dtypes.bfloat16).astype(np.float64), axis, -1)
    blocks = v.reshape(v.shape[:-1] + (-1, 32))
    amax = np.abs(blocks).max(-1, keepdims=True)
    byte = np.maximum(np.where(amax > 0, np.frexp(amax)[1] - 1 + 127, 0) - down, 1)
    scale = np.exp2(byte - 127.0)
    codes = (blocks / scale).astype(np.float32).astype(dtype).astype(np.float64)
    return np.moveaxis((codes * scale).reshape(v.shape), -1, axis)


WIDE = False


def mx_kscale(k):
    if not WIDE:
        return np.ones(k)
    levels = np.array([10, -10, 5, -5, 0])
    a = np.random.permutation(np.resize(levels, k // 512 * 4)).reshape(k // 512, 4)
    idx = np.arange(k)
    return np.exp2(a[idx // 512, idx % 128 // 32])


BF16 = ml_dtypes.bfloat16


def bf(x):
    return np.asarray(x, np.float32).astype(BF16)


def f64(x):
    return np.asarray(x).astype(np.float64)


E2M1 = np.array([0.0, 0.5, 1.0, 1.5, 2.0, 3.0, 4.0, 6.0, -0.0, -0.5, -1.0, -1.5, -2.0, -3.0, -4.0, -6.0])


def pack_weight(w, fmt):
    k, n = w.shape
    w = f64(bf(w)).reshape(k // 32, 32, n)
    amax = np.abs(w).max(1)
    if fmt == "e4m3":
        byte = np.frexp(amax)[1] - 1 + 127 - 7
    else:
        mant, ex = np.frexp(amax / 6.0)
        byte = np.where(mant > 0.5, ex, ex - 1) + 127
    byte = np.clip(np.where(amax > 0, byte, 1), 1, 254)
    scaled = (w * np.exp2(127.0 - byte)[:, None, :]).reshape(k, n).astype(np.float32)
    by_word = np.ascontiguousarray(scaled.reshape(k // 512, 128, 4, n).transpose(0, 1, 3, 2))
    if fmt == "e4m3":
        words = by_word.astype(ml_dtypes.float8_e4m3fn).view(np.uint8)
    else:
        c = by_word.astype(ml_dtypes.float4_e2m1fn).view(np.uint8) & 0xF
        words = c[..., 0::2] | (c[..., 1::2] << 4)
    return np.ascontiguousarray(words), np.ascontiguousarray(byte.astype(np.uint8).reshape(k // 512, 16, n))


def unpack_weight(words, scales, fmt):
    g, p, n, _ = words.shape
    if fmt == "e4m3":
        vals = np.ascontiguousarray(words).view(ml_dtypes.float8_e4m3fn).astype(np.float64)
    else:
        nib = np.empty((g, p, n, 4), np.uint8)
        nib[..., 0::2] = words & 0xF
        nib[..., 1::2] = words >> 4
        vals = E2M1[nib]
    vals = vals * np.repeat(np.exp2(scales.astype(np.float64) - 127.0), 8, axis=1)[..., None]
    return vals.transpose(0, 1, 3, 2).reshape(g * 512, n)

def pack4(w):
    words, scales = pack_weight(w, "e2m1")
    return words.reshape(words.shape[0], 128, -1), scales


def unpack4(words, scales):
    return unpack_weight(words.reshape(words.shape[0], 128, -1, 2), scales, "e2m1")


B, C, CK, CV, CO, H, W, P1, P2, P3, P4 = 2, 1024, 1024, 128, 1024, 48, 48, 1, 3, 6, 8
PSP_SIZES = (P1, P2, P3, P4)
EPS = 1e-5
N = H * W


def bnrelu(x, gamma, beta, mean, var):
    inv = 1.0 / np.sqrt(var + EPS)
    return np.maximum((x - mean[None, :, None]) * (inv * gamma)[None, :, None] + beta[None, :, None], 0.0)


def psp(x):
    b, c = x.shape[:2]
    outs = []
    for s in PSP_SIZES:
        outs.append(x.reshape(b, c, s, H // s, s, W // s).mean(axis=(3, 5)).reshape(b, c, s * s))
    return np.concatenate(outs, axis=-1)


def setup_inputs():
    s = mx_kscale(C)
    fine = np.random.standard_normal((B, C, H, W))
    coarse = np.random.standard_normal((B, C, P4, P4))
    coarse = np.repeat(np.repeat(coarse, H // P4, axis=2), W // P4, axis=3)
    feats = bf((fine + coarse) * np.sqrt(0.5) * s[None, :, None, None])
    wk = np.random.standard_normal((CK, C)) * 1.5 / np.sqrt(C) / s[None, :]
    bk = bf(np.random.standard_normal(CK) * 0.2)
    gk = bf(1.0 + 0.1 * np.random.standard_normal(CK))
    betak = bf(np.random.standard_normal(CK) * 0.2)
    mk = bf(np.random.standard_normal(CK) * 0.2)
    vk = bf(np.random.uniform(0.5, 1.5, CK))
    wv = np.random.standard_normal((CV, C)) / np.sqrt(C) / s[None, :]
    bv = bf(np.random.standard_normal(CV) * 0.2)
    wk_words, wk_scales = pack4(np.ascontiguousarray(wk.T))
    wv_words, wv_scales = pack4(np.ascontiguousarray(wv.T))
    return {"feats": feats,
            "Wk_words": wk_words,
            "Wk_scales": wk_scales,
            "bk": bk,
            "gk": gk,
            "betak": betak,
            "mk": mk,
            "vk": vk,
            "Wv_words": wv_words,
            "Wv_scales": wv_scales,
            "bv": bv}


def reference(feats, Wk_words, Wk_scales, bk, gk, betak, mk, vk, Wv_words, Wv_scales, bv):
    xq = mxq(f64(feats).reshape(B, C, N), 1, "e4m3")
    pre = (unpack4(Wk_words, Wk_scales).T @ xq) + f64(bk)[None, :, None]
    kf = bnrelu(pre, f64(gk), f64(betak), f64(mk), f64(vk)).reshape(B, CK, H, W)
    keyp = psp(kf)
    val = ((unpack4(Wv_words, Wv_scales).T @ xq) + f64(bv)[None, :, None]).reshape(B, CV, H, W)
    value = psp(val).transpose(0, 2, 1)
    return kf, keyp, value

@@ -1,0 +1,263 @@
+from contextlib import ExitStack
+
+import concourse.mybir as mybir
+from concourse.masks import make_identity
+
+F32 = mybir.dt.float32
+BF16 = mybir.dt.bfloat16
+U8 = mybir.dt.uint8
+U32 = mybir.dt.uint32
+I32 = mybir.dt.int32
+FP8X4 = mybir.dt.float8_e4m3fn_x4
+FP4X4 = mybir.dt.float4_e2m1fn_x4
+ACT = mybir.ActivationFunctionType
+ALU = mybir.AluOpType
+AXIS = mybir.AxisListType
+
+P = 128
+PACK = 4
+K_PASS = P * PACK
+IMAGES = 2
+CHANNELS = 1024
+PASSES = CHANNELS // K_PASS
+SIDE = 48
+IMAGE_POS = SIDE * SIDE
+POSITIONS = IMAGES * IMAGE_POS
+KEY_TILES = 8
+VALUE_TILE = 8
+OUT_TILES = KEY_TILES + 1
+OUT_CHANNELS = OUT_TILES * P
+N_TILE = 512
+STRIPE_TILES = 3
+STRIPE = STRIPE_TILES * N_TILE
+STRIPES = POSITIONS // STRIPE
+UNITS = STRIPE_TILES * PASSES
+SCALAR_COLS = 384
+HALF = SIDE // 2
+GRID = HALF * HALF
+STRIPE_GRID = STRIPE // 4
+TOKENS = 110
+EPS = 1e-5
+
+FLOPS = 2 * POSITIONS * CHANNELS * OUT_CHANNELS
+
+ROW_BK, ROW_GK, ROW_BETAK, ROW_MK, ROW_VK, ROW_BV = 0, 8, 16, 24, 32, 40
+
+
+def image_runs(first, count):
+    runs = []
+    for image in range(IMAGES):
+        lo = max(first, image * IMAGE_POS)
+        hi = min(first + count, (image + 1) * IMAGE_POS)
+        if lo < hi:
+            runs.append((image, lo - image * IMAGE_POS, lo - first, hi - lo))
+    return runs
+
+
+def tile_apnb_pa_t_kernel(
+    tc, feats, Wk_words, Wk_scales, bk, gk, betak, mk, vk, Wv_words, Wv_scales, bv, out_0, out_1, out_2
+):
+    nc = tc.nc
+    feats_rows = feats.rearrange("b (g p j) h w -> b g p j (h w)", g=PASSES, p=P, j=PACK)
+    kf_out = out_0.rearrange("b c h w -> b c (h w)")
+
+    with ExitStack() as ctx:
+        keep = ctx.enter_context(tc.tile_pool(name="keep", bufs=1))
+        raw_pool = ctx.enter_context(tc.tile_pool(name="raw", bufs=4))
+        grouped_pool = ctx.enter_context(tc.tile_pool(name="grouped", bufs=3))
+        kf_pool = ctx.enter_context(tc.tile_pool(name="kf", bufs=6))
+        pair_pool = ctx.enter_context(tc.tile_pool(name="pairs", bufs=2))
+        acc_pool = ctx.enter_context(tc.psum_pool(name="acc", bufs=7))
+        flip_pool = ctx.enter_context(tc.psum_pool(name="flip", bufs=1))
+
+        w_words = keep.tile([P, PASSES, 2 * OUT_CHANNELS], U8, align_bytes=64)
+        w_scales = keep.tile([P, PASSES, OUT_CHANNELS], U8, align_bytes=64)
+        x_codes = keep.tile([P, PASSES, POSITIONS], U32, align_bytes=64)
+        x_scales = keep.tile([P, PASSES, POSITIONS], U8, align_bytes=64)
+        grid = keep.tile([P, OUT_TILES, IMAGES * GRID], F32)
+        sum8 = keep.tile([P, IMAGES, OUT_TILES, 64], F32)
+        sum6 = keep.tile([P, IMAGES, OUT_TILES, 36], F32)
+        sum3 = keep.tile([P, IMAGES, OUT_TILES, 9], F32)
+        sum1 = keep.tile([P, IMAGES, OUT_TILES, 1], F32)
+        tokens = keep.tile([P, IMAGES, OUT_TILES, P], F32)
+        scale_all = keep.tile([P, OUT_TILES], F32)
+        shift_all = keep.tile([P, OUT_TILES], F32)
+
+        def load_stripe(stripe):
+            tiles = []
+            for g in range(PASSES):
+                raw = raw_pool.tile([P, PACK, STRIPE], BF16)
+                for image, start, offset, width in image_runs(stripe * STRIPE, STRIPE):
+                    nc.sync.dma_start(
+                        out=raw[:, :, offset : offset + width],
+                        in_=feats_rows[image, g, :, :, start : start + width],
+                    )
+                tiles.append(raw)
+            return tiles
+
+        rows_bf = keep.tile([P, P], BF16)
+        nc.vector.memset(rows_bf[:], 0.0)
+        for vector, row in ((bk, ROW_BK), (gk, ROW_GK), (betak, ROW_BETAK), (mk, ROW_MK), (vk, ROW_VK), (bv, ROW_BV)):
+            blocks = vector.rearrange("(m c) -> m c", c=P)
+            nc.scalar.dma_start(out=rows_bf[row : row + blocks.shape[0], :], in_=blocks)
+        raw_tiles = {0: load_stripe(0)}
+
+        nc.vector.memset(w_scales[:].rearrange("p g n -> p (g n)").bitcast(I32), 0)
+        for scales, first, width in ((Wk_scales, 0, KEY_TILES * P), (Wv_scales, KEY_TILES * P, P)):
+            for quadrant in range(4):
+                nc.sync.dma_start(
+                    out=w_scales[32 * quadrant : 32 * quadrant + 4, :, first : first + width].bitcast(I32),
+                    in_=scales[:, 4 * quadrant : 4 * quadrant + 4, :].rearrange("g r n -> r g n").bitcast(I32),
+                )
+        for words, first, width in ((Wk_words, 0, 2 * KEY_TILES * P), (Wv_words, 2 * KEY_TILES * P, 2 * P)):
+            nc.sync.dma_start(
+                out=w_words[:, :, first : first + width].bitcast(I32),
+                in_=words.rearrange("g p n -> p g n").bitcast(I32),
+            )
+        raw_tiles[1] = load_stripe(1)
+
+        identity = keep.tile([P, P], F32)
+        make_identity(nc, identity[:])
+        rows_f32 = keep.tile([P, P], F32)
+        nc.vector.tensor_copy(out=rows_f32[:], in_=rows_bf[:])
+        flipped = flip_pool.tile([P, P], F32)
+        nc.tensor.transpose(flipped[:], rows_f32[:], identity[:])
+        par = keep.tile([P, P], F32)
+        nc.vector.tensor_copy(out=par[:], in_=flipped[:])
+
+        def par_cols(row):
+            return par[:, row : row + KEY_TILES]
+
+        key_scale = scale_all[:, 0:KEY_TILES]
+        key_shift = shift_all[:, 0:KEY_TILES]
+        spread = keep.tile([P, KEY_TILES], F32)
+        nc.vector.tensor_scalar_add(out=spread[:], in0=par_cols(ROW_VK), scalar1=EPS)
+        nc.scalar.sqrt(out=spread[:], in_=spread[:])
+        nc.vector.reciprocal(out=spread[:], in_=spread[:])
+        nc.vector.tensor_mul(out=key_scale, in0=par_cols(ROW_GK), in1=spread[:])
+        nc.vector.tensor_sub(out=key_shift, in0=par_cols(ROW_BK), in1=par_cols(ROW_MK))
+        nc.vector.tensor_mul(out=key_shift, in0=key_shift, in1=key_scale)
+        nc.vector.tensor_add(out=key_shift, in0=key_shift, in1=par_cols(ROW_BETAK))
+        nc.vector.memset(scale_all[:, VALUE_TILE : VALUE_TILE + 1], 1.0)
+        nc.vector.tensor_copy(out=shift_all[:, VALUE_TILE : VALUE_TILE + 1], in_=par[:, ROW_BV : ROW_BV + 1])
+        nc.vector.memset(tokens[:, :, VALUE_TILE, TOKENS:P], 0.0)
+
+        def quantise_unit(stripe, unit):
+            n_tile, g = divmod(unit, PASSES)
+            raw = raw_tiles[stripe][g]
+            grouped = grouped_pool.tile([P, N_TILE, PACK], BF16, align_bytes=64)
+            for copy, lo, hi in ((nc.scalar.copy, 0, SCALAR_COLS), (nc.vector.tensor_copy, SCALAR_COLS, N_TILE)):
+                copy(
+                    out=grouped[:, lo:hi, :].rearrange("p (c i) j -> p c j i", i=4),
+                    in_=raw[:, :, n_tile * N_TILE + lo : n_tile * N_TILE + hi].rearrange("p j (c i) -> p c j i", i=4),
+                )
+            cols = slice(stripe * STRIPE + n_tile * N_TILE, stripe * STRIPE + (n_tile + 1) * N_TILE)
+            nc.vector.quantize_mx(
+                out=x_codes[:, g, cols].bitcast(FP8X4),
+                scales=x_scales[:, g, cols],
+                in_=grouped[:].rearrange("p c j -> p (c j)"),
+            )
+
+        def project(stripe, m):
+            kf = kf_pool.tile([P, STRIPE], F32)
+            for n_tile in range(STRIPE_TILES):
+                cols = slice(stripe * STRIPE + n_tile * N_TILE, stripe * STRIPE + (n_tile + 1) * N_TILE)
+                acc = acc_pool.tile([P, N_TILE], F32)
+                for g in range(PASSES):
+                    nc.tensor.matmul_mx(
+                        out=acc[:],
+                        lhsT=w_words[:, g, 2 * P * m : 2 * P * (m + 1)].bitcast(FP4X4),
+                        lhsT_scale=w_scales[:, g, P * m : P * (m + 1)],
+                        rhs=x_codes[:, g, cols].bitcast(FP8X4),
+                        rhs_scale=x_scales[:, g, cols],
+                        start=(g == 0),
+                        stop=(g == PASSES - 1),
+                    )
+                nc.scalar.activation(
+                    out=kf[:, n_tile * N_TILE : (n_tile + 1) * N_TILE],
+                    in_=acc[:],
+                    func=ACT.Relu if m < KEY_TILES else ACT.Identity,
+                    bias=shift_all[:, m : m + 1],
+                    scale=scale_all[:, m : m + 1],
+                )
+            if m < KEY_TILES:
+                for image, start, offset, width in image_runs(stripe * STRIPE, STRIPE):
+                    nc.sync.dma_start(
+                        out=kf_out[image, P * m : P * (m + 1), start : start + width],
+                        in_=kf[:, offset : offset + width],
+                    )
+            return kf
+
+        def sum_2x2(stripe, m, kf):
+            rows = kf[:].rearrange("p (r two w) -> p r two w", two=2, w=SIDE)
+            row_pairs = pair_pool.tile([P, STRIPE // 2], F32)
+            nc.vector.tensor_tensor(
+                out=row_pairs[:].rearrange("p (r w) -> p r w", w=SIDE),
+                in0=rows[:, :, 0, :],
+                in1=rows[:, :, 1, :],
+                op=ALU.add,
+            )
+            cols = row_pairs[:].rearrange("p (c two) -> p c two", two=2)
+            nc.vector.tensor_tensor(
+                out=grid[:, m, stripe * STRIPE_GRID : (stripe + 1) * STRIPE_GRID],
+                in0=cols[:, :, 0],
+                in1=cols[:, :, 1],
+                op=ALU.add,
+            )
+
+        def sum_cells(image, m):
+            squares = grid[:, m, image * GRID : (image + 1) * GRID]
+            for sums, cells in ((sum8, 8), (sum6, 6)):
+                nc.vector.tensor_reduce(
+                    out=sums[:, image, m, :],
+                    in_=squares.rearrange(
+                        "p (bh i bw j) -> p bh bw i j", bh=cells, i=HALF // cells, bw=cells, j=HALF // cells
+                    ),
+                    axis=AXIS.XY,
+                    op=ALU.add,
+                )
+
+        def finish_image(image):
+            nc.vector.tensor_reduce(
+                out=sum3[:, image],
+                in_=sum6[:, image]
+                .rearrange("p m c -> p (m c)")
+                .rearrange("p (mb i bw j) -> p mb bw i j", i=2, bw=3, j=2),
+                axis=AXIS.XY,
+                op=ALU.add,
+            )
+            nc.vector.tensor_reduce(out=sum1[:, image], in_=sum3[:, image], axis=AXIS.X, op=ALU.add)
+            first = 0
+            for sums, cells in ((sum1, 1), (sum3, 3), (sum6, 6), (sum8, 8)):
+                nc.vector.tensor_scalar_mul(
+                    out=tokens[:, image, :, first : first + cells * cells],
+                    in0=sums[:, image],
+                    scalar1=float(cells * cells) / IMAGE_POS,
+                )
+                first += cells * cells
+            nc.sync.dma_start(
+                out=out_1[image].rearrange("(m p) t -> p m t", p=P),
+                in_=tokens[:, image, 0:KEY_TILES, 0:TOKENS],
+            )
+            flipped = flip_pool.tile([P, P], F32)
+            nc.tensor.transpose(flipped[:], tokens[:, image, VALUE_TILE, :], identity[:])
+            value = pair_pool.tile([P, P], F32)
+            nc.vector.tensor_copy(out=value[:], in_=flipped[:])
+            nc.sync.dma_start(out=out_2[image], in_=value[0:TOKENS, :])
+
+        for unit in range(UNITS):
+            quantise_unit(0, unit)
+        for stripe in range(STRIPES):
+            if stripe + 2 < STRIPES:
+                raw_tiles[stripe + 2] = load_stripe(stripe + 2)
+            last_col = (stripe + 1) * STRIPE
+            done_image = last_col // IMAGE_POS - 1 if last_col % IMAGE_POS < STRIPE else None
+            for m in range(OUT_TILES):
+                kf = project(stripe, m)
+                sum_2x2(stripe, m, kf)
+                if done_image is not None:
+                    sum_cells(done_image, m)
+                if stripe + 1 < STRIPES and m < UNITS:
+                    quantise_unit(stripe + 1, m)
+            if done_image is not None:
+                finish_image(done_image)

@@ -28,30 +28,23 @@ VALUE_TILE = 8
 OUT_TILES = KEY_TILES + 1
 OUT_CHANNELS = OUT_TILES * P
 N_TILE = 512
-STRIPE_TILES = 3
-STRIPE = STRIPE_TILES * N_TILE
-STRIPES = POSITIONS // STRIPE
-UNITS = STRIPE_TILES * PASSES
-SCALAR_COLS = 384
-HALF = SIDE // 2
-GRID = HALF * HALF
+STRIPE_ROWS = 24
+STRIPE = STRIPE_ROWS * SIDE
+IMAGE_STRIPES = IMAGE_POS // STRIPE
+STRIPES = IMAGES * IMAGE_STRIPES
+N_TILES = ((0, N_TILE), (N_TILE, N_TILE), (2 * N_TILE, STRIPE - 2 * N_TILE))
+UNITS = len(N_TILES) * PASSES
+GROUP = 3
 STRIPE_GRID = STRIPE // 4
+HALF = SIDE // 2
+LANE_COLS = 256
 TOKENS = 110
+FIRST_TOKEN = {1: 0, 3: 1, 6: 10, 8: 46}
 EPS = 1e-5
 
 FLOPS = 2 * POSITIONS * CHANNELS * OUT_CHANNELS
 
 ROW_BK, ROW_GK, ROW_BETAK, ROW_MK, ROW_VK, ROW_BV = 0, 8, 16, 24, 32, 40
-
-
-def image_runs(first, count):
-    runs = []
-    for image in range(IMAGES):
-        lo = max(first, image * IMAGE_POS)
-        hi = min(first + count, (image + 1) * IMAGE_POS)
-        if lo < hi:
-            runs.append((image, lo - image * IMAGE_POS, lo - first, hi - lo))
-    return runs
 
 
 def tile_apnb_pa_t_kernel(
@@ -63,18 +56,17 @@ def tile_apnb_pa_t_kernel(
 
     with ExitStack() as ctx:
         keep = ctx.enter_context(tc.tile_pool(name="keep", bufs=1))
-        raw_pool = ctx.enter_context(tc.tile_pool(name="raw", bufs=4))
         grouped_pool = ctx.enter_context(tc.tile_pool(name="grouped", bufs=3))
-        kf_pool = ctx.enter_context(tc.tile_pool(name="kf", bufs=6))
-        pair_pool = ctx.enter_context(tc.tile_pool(name="pairs", bufs=2))
-        acc_pool = ctx.enter_context(tc.psum_pool(name="acc", bufs=7))
-        flip_pool = ctx.enter_context(tc.psum_pool(name="flip", bufs=1))
+        kf_pool = ctx.enter_context(tc.tile_pool(name="kf", bufs=8))
+        pool_pool = ctx.enter_context(tc.tile_pool(name="pooling", bufs=2))
+        acc_pool = ctx.enter_context(tc.psum_pool(name="acc", bufs=6))
+        lane_pool = ctx.enter_context(tc.psum_pool(name="lanes", bufs=2))
+        ctx.enter_context(tc.manual_schedule())
 
         w_words = keep.tile([P, PASSES, 2 * OUT_CHANNELS], U8, align_bytes=64)
         w_scales = keep.tile([P, PASSES, OUT_CHANNELS], U8, align_bytes=64)
         x_codes = keep.tile([P, PASSES, POSITIONS], U32, align_bytes=64)
         x_scales = keep.tile([P, PASSES, POSITIONS], U8, align_bytes=64)
-        grid = keep.tile([P, OUT_TILES, IMAGES * GRID], F32)
         sum8 = keep.tile([P, IMAGES, OUT_TILES, 64], F32)
         sum6 = keep.tile([P, IMAGES, OUT_TILES, 36], F32)
         sum3 = keep.tile([P, IMAGES, OUT_TILES, 9], F32)
@@ -84,43 +76,54 @@ def tile_apnb_pa_t_kernel(
         shift_all = keep.tile([P, OUT_TILES], F32)
 
         def load_stripe(stripe):
-            tiles = []
-            for g in range(PASSES):
-                raw = raw_pool.tile([P, PACK, STRIPE], BF16)
-                for image, start, offset, width in image_runs(stripe * STRIPE, STRIPE):
+            image, part = divmod(stripe, IMAGE_STRIPES)
+            tiles = [keep.tile([P, PACK, STRIPE], BF16, name="raw%d_%d" % (stripe, g)) for g in range(PASSES)]
+            for first, width in N_TILES if stripe == 0 else ((0, STRIPE),):
+                for g in range(PASSES):
                     nc.sync.dma_start(
-                        out=raw[:, :, offset : offset + width],
-                        in_=feats_rows[image, g, :, :, start : start + width],
+                        out=tiles[g][:, :, first : first + width],
+                        in_=feats_rows[image, g, :, :, part * STRIPE + first : part * STRIPE + first + width],
                     )
-                tiles.append(raw)
             return tiles
 
-        rows_bf = keep.tile([P, P], BF16)
-        nc.vector.memset(rows_bf[:], 0.0)
-        for vector, row in ((bk, ROW_BK), (gk, ROW_GK), (betak, ROW_BETAK), (mk, ROW_MK), (vk, ROW_VK), (bv, ROW_BV)):
-            blocks = vector.rearrange("(m c) -> m c", c=P)
-            nc.scalar.dma_start(out=rows_bf[row : row + blocks.shape[0], :], in_=blocks)
-        raw_tiles = {0: load_stripe(0)}
-
-        nc.vector.memset(w_scales[:].rearrange("p g n -> p (g n)").bitcast(I32), 0)
-        for scales, first, width in ((Wk_scales, 0, KEY_TILES * P), (Wv_scales, KEY_TILES * P, P)):
+        def load_scales(scales, first, width):
             for quadrant in range(4):
                 nc.sync.dma_start(
                     out=w_scales[32 * quadrant : 32 * quadrant + 4, :, first : first + width].bitcast(I32),
                     in_=scales[:, 4 * quadrant : 4 * quadrant + 4, :].rearrange("g r n -> r g n").bitcast(I32),
                 )
-        for words, first, width in ((Wk_words, 0, 2 * KEY_TILES * P), (Wv_words, 2 * KEY_TILES * P, 2 * P)):
+
+        def load_words(words, first, width):
             nc.sync.dma_start(
                 out=w_words[:, :, first : first + width].bitcast(I32),
                 in_=words.rearrange("g p n -> p g n").bitcast(I32),
             )
-        raw_tiles[1] = load_stripe(1)
+
+        warm = keep.tile([P, 1], F32)
+        nc.vector.memset(warm[:], 1.0)
+        nc.scalar.sqrt(out=warm[:], in_=warm[:])
+        rows_bf = keep.tile([P, P], BF16)
+        nc.vector.memset(rows_bf[:], 0.0)
+        for vector, row in ((bk, ROW_BK), (gk, ROW_GK), (betak, ROW_BETAK), (mk, ROW_MK), (vk, ROW_VK), (bv, ROW_BV)):
+            blocks = vector.rearrange("(m c) -> m c", c=P)
+            nc.scalar.dma_start(out=rows_bf[row : row + blocks.shape[0], :], in_=blocks)
+        nc.vector.memset(w_scales[:].rearrange("p g n -> p (g n)").bitcast(I32), 0)
+        raw_tiles = [load_stripe(0)]
+        load_scales(Wk_scales, 0, KEY_TILES * P)
+        load_words(Wk_words, 0, 2 * KEY_TILES * P)
+        load_words(Wv_words, 2 * KEY_TILES * P, 2 * P)
+        raw_tiles.append(load_stripe(1))
+        load_scales(Wv_scales, KEY_TILES * P, P)
+        raw_tiles.append(load_stripe(2))
+        raw_tiles.append(load_stripe(3))
 
         identity = keep.tile([P, P], F32)
         make_identity(nc, identity[:])
+        identity_bf = keep.tile([P, P], BF16)
+        make_identity(nc, identity_bf[:])
         rows_f32 = keep.tile([P, P], F32)
         nc.vector.tensor_copy(out=rows_f32[:], in_=rows_bf[:])
-        flipped = flip_pool.tile([P, P], F32)
+        flipped = lane_pool.tile([P, P], F32, tag="lanes")
         nc.tensor.transpose(flipped[:], rows_f32[:], identity[:])
         par = keep.tile([P, P], F32)
         nc.vector.tensor_copy(out=par[:], in_=flipped[:])
@@ -140,32 +143,57 @@ def tile_apnb_pa_t_kernel(
         nc.vector.tensor_add(out=key_shift, in0=key_shift, in1=par_cols(ROW_BETAK))
         nc.vector.memset(scale_all[:, VALUE_TILE : VALUE_TILE + 1], 1.0)
         nc.vector.tensor_copy(out=shift_all[:, VALUE_TILE : VALUE_TILE + 1], in_=par[:, ROW_BV : ROW_BV + 1])
-        nc.vector.memset(tokens[:, :, VALUE_TILE, TOKENS:P], 0.0)
+        nc.vector.memset(tokens[:, :, VALUE_TILE, :], 0.0)
 
-        def quantise_unit(stripe, unit):
+        def regroup_unit(stripe, unit):
             n_tile, g = divmod(unit, PASSES)
+            first, width = N_TILES[n_tile]
             raw = raw_tiles[stripe][g]
             grouped = grouped_pool.tile([P, N_TILE, PACK], BF16, align_bytes=64)
-            for copy, lo, hi in ((nc.scalar.copy, 0, SCALAR_COLS), (nc.vector.tensor_copy, SCALAR_COLS, N_TILE)):
-                copy(
-                    out=grouped[:, lo:hi, :].rearrange("p (c i) j -> p c j i", i=4),
-                    in_=raw[:, :, n_tile * N_TILE + lo : n_tile * N_TILE + hi].rearrange("p j (c i) -> p c j i", i=4),
+            if width == N_TILE:
+                for lo in range(0, width, LANE_COLS):
+                    lanes = lane_pool.tile([P, LANE_COLS, PACK], BF16, tag="lanes")
+                    for j in range(0, PACK, 2):
+                        nc.tensor.matmul(
+                            out=lanes[:, :, j : j + 2].rearrange("p c j -> p j c"),
+                            lhsT=identity_bf[:],
+                            rhs=raw[:, j : j + 2, first + lo : first + lo + LANE_COLS],
+                            start=True,
+                            stop=True,
+                        )
+                    nc.scalar.copy(out=grouped[:, lo : lo + LANE_COLS, :], in_=lanes[:])
+            else:
+                nc.vector.tensor_copy(
+                    out=grouped[:, 0:width, :].rearrange("p (c i) j -> p c j i", i=4),
+                    in_=raw[:, :, first : first + width].rearrange("p j (c i) -> p c j i", i=4),
                 )
-            cols = slice(stripe * STRIPE + n_tile * N_TILE, stripe * STRIPE + (n_tile + 1) * N_TILE)
+            return grouped
+
+        def quantise_unit(stripe, unit, grouped):
+            n_tile, g = divmod(unit, PASSES)
+            first, width = N_TILES[n_tile]
+            cols = slice(stripe * STRIPE + first, stripe * STRIPE + first + width)
             nc.vector.quantize_mx(
                 out=x_codes[:, g, cols].bitcast(FP8X4),
                 scales=x_scales[:, g, cols],
-                in_=grouped[:].rearrange("p c j -> p (c j)"),
+                in_=grouped[:, 0:width, :].rearrange("p c j -> p (c j)"),
             )
 
+        def prepare_step(stripe, step, waiting):
+            if step < UNITS:
+                waiting.append(regroup_unit(stripe, step))
+            if 0 < step <= UNITS:
+                quantise_unit(stripe, step - 1, waiting[step - 1])
+
         def project(stripe, m):
+            image, part = divmod(stripe, IMAGE_STRIPES)
             kf = kf_pool.tile([P, STRIPE], F32)
-            for n_tile in range(STRIPE_TILES):
-                cols = slice(stripe * STRIPE + n_tile * N_TILE, stripe * STRIPE + (n_tile + 1) * N_TILE)
+            for first, width in N_TILES:
+                cols = slice(stripe * STRIPE + first, stripe * STRIPE + first + width)
                 acc = acc_pool.tile([P, N_TILE], F32)
                 for g in range(PASSES):
                     nc.tensor.matmul_mx(
-                        out=acc[:],
+                        out=acc[:, 0:width],
                         lhsT=w_words[:, g, 2 * P * m : 2 * P * (m + 1)].bitcast(FP4X4),
                         lhsT_scale=w_scales[:, g, P * m : P * (m + 1)],
                         rhs=x_codes[:, g, cols].bitcast(FP8X4),
@@ -174,50 +202,43 @@ def tile_apnb_pa_t_kernel(
                         stop=(g == PASSES - 1),
                     )
                 nc.scalar.activation(
-                    out=kf[:, n_tile * N_TILE : (n_tile + 1) * N_TILE],
-                    in_=acc[:],
+                    out=kf[:, first : first + width],
+                    in_=acc[:, 0:width],
                     func=ACT.Relu if m < KEY_TILES else ACT.Identity,
                     bias=shift_all[:, m : m + 1],
                     scale=scale_all[:, m : m + 1],
                 )
             if m < KEY_TILES:
-                for image, start, offset, width in image_runs(stripe * STRIPE, STRIPE):
-                    nc.sync.dma_start(
-                        out=kf_out[image, P * m : P * (m + 1), start : start + width],
-                        in_=kf[:, offset : offset + width],
-                    )
+                nc.sync.dma_start(
+                    out=kf_out[image, P * m : P * (m + 1), part * STRIPE : (part + 1) * STRIPE], in_=kf[:]
+                )
             return kf
 
-        def sum_2x2(stripe, m, kf):
+        def add_row_pairs(kf, row_pairs, slot):
             rows = kf[:].rearrange("p (r two w) -> p r two w", two=2, w=SIDE)
-            row_pairs = pair_pool.tile([P, STRIPE // 2], F32)
             nc.vector.tensor_tensor(
-                out=row_pairs[:].rearrange("p (r w) -> p r w", w=SIDE),
+                out=row_pairs[:, slot, :].rearrange("p (r w) -> p r w", w=SIDE),
                 in0=rows[:, :, 0, :],
                 in1=rows[:, :, 1, :],
                 op=ALU.add,
             )
-            cols = row_pairs[:].rearrange("p (c two) -> p c two", two=2)
-            nc.vector.tensor_tensor(
-                out=grid[:, m, stripe * STRIPE_GRID : (stripe + 1) * STRIPE_GRID],
-                in0=cols[:, :, 0],
-                in1=cols[:, :, 1],
-                op=ALU.add,
-            )
 
-        def sum_cells(image, m):
-            squares = grid[:, m, image * GRID : (image + 1) * GRID]
+        def pool_group(stripe, m_first, row_pairs):
+            image, part = divmod(stripe, IMAGE_STRIPES)
+            col_pairs = row_pairs[:].rearrange("p m (c two) -> p (m c) two", two=2)
+            squares = pool_pool.tile([P, GROUP * STRIPE_GRID], F32)
+            nc.vector.tensor_tensor(out=squares[:], in0=col_pairs[:, :, 0], in1=col_pairs[:, :, 1], op=ALU.add)
             for sums, cells in ((sum8, 8), (sum6, 6)):
+                side = HALF // cells
+                here = cells * cells // IMAGE_STRIPES
                 nc.vector.tensor_reduce(
-                    out=sums[:, image, m, :],
-                    in_=squares.rearrange(
-                        "p (bh i bw j) -> p bh bw i j", bh=cells, i=HALF // cells, bw=cells, j=HALF // cells
-                    ),
+                    out=sums[:, image, m_first : m_first + GROUP, part * here : (part + 1) * here],
+                    in_=squares[:].rearrange("p (mb i bw j) -> p mb bw i j", i=side, bw=cells, j=side),
                     axis=AXIS.XY,
                     op=ALU.add,
                 )
 
-        def finish_image(image):
+        def sum_coarse_levels(image):
             nc.vector.tensor_reduce(
                 out=sum3[:, image],
                 in_=sum6[:, image]
@@ -227,37 +248,39 @@ def tile_apnb_pa_t_kernel(
                 op=ALU.add,
             )
             nc.vector.tensor_reduce(out=sum1[:, image], in_=sum3[:, image], axis=AXIS.X, op=ALU.add)
-            first = 0
-            for sums, cells in ((sum1, 1), (sum3, 3), (sum6, 6), (sum8, 8)):
-                nc.vector.tensor_scalar_mul(
-                    out=tokens[:, image, :, first : first + cells * cells],
-                    in0=sums[:, image],
-                    scalar1=float(cells * cells) / IMAGE_POS,
+
+        def store_tokens(image):
+            for sums, cells in ((sum8, 8), (sum6, 6), (sum3, 3), (sum1, 1)):
+                nc.scalar.mul(
+                    out=tokens[:, image, :, FIRST_TOKEN[cells] : FIRST_TOKEN[cells] + cells * cells],
+                    in_=sums[:, image],
+                    mul=float(cells * cells) / IMAGE_POS,
                 )
-                first += cells * cells
             nc.sync.dma_start(
                 out=out_1[image].rearrange("(m p) t -> p m t", p=P),
                 in_=tokens[:, image, 0:KEY_TILES, 0:TOKENS],
             )
-            flipped = flip_pool.tile([P, P], F32)
+            flipped = lane_pool.tile([P, P], F32, tag="lanes")
             nc.tensor.transpose(flipped[:], tokens[:, image, VALUE_TILE, :], identity[:])
-            value = pair_pool.tile([P, P], F32)
-            nc.vector.tensor_copy(out=value[:], in_=flipped[:])
+            value = pool_pool.tile([P, P], F32)
+            nc.scalar.copy(out=value[:], in_=flipped[:])
             nc.sync.dma_start(out=out_2[image], in_=value[0:TOKENS, :])
 
-        for unit in range(UNITS):
-            quantise_unit(0, unit)
+        waiting = []
+        for step in range(UNITS + 1):
+            prepare_step(0, step, waiting)
         for stripe in range(STRIPES):
-            if stripe + 2 < STRIPES:
-                raw_tiles[stripe + 2] = load_stripe(stripe + 2)
-            last_col = (stripe + 1) * STRIPE
-            done_image = last_col // IMAGE_POS - 1 if last_col % IMAGE_POS < STRIPE else None
+            waiting = []
             for m in range(OUT_TILES):
                 kf = project(stripe, m)
-                sum_2x2(stripe, m, kf)
-                if done_image is not None:
-                    sum_cells(done_image, m)
-                if stripe + 1 < STRIPES and m < UNITS:
-                    quantise_unit(stripe + 1, m)
-            if done_image is not None:
-                finish_image(done_image)
+                if stripe + 1 < STRIPES:
+                    prepare_step(stripe + 1, m, waiting)
+                if m % GROUP == 0:
+                    row_pairs = pool_pool.tile([P, GROUP, STRIPE // 2], F32)
+                add_row_pairs(kf, row_pairs, m % GROUP)
+                if m % GROUP == GROUP - 1:
+                    pool_group(stripe, m - GROUP + 1, row_pairs)
+            if stripe % IMAGE_STRIPES == IMAGE_STRIPES - 1:
+                sum_coarse_levels(stripe // IMAGE_STRIPES)
+        for image in range(IMAGES):
+            store_tokens(image)

@@ -37,7 +37,8 @@ UNITS = len(N_TILES) * PASSES
 GROUP = 3
 STRIPE_GRID = STRIPE // 4
 HALF = SIDE // 2
-LANE_COLS = 256
+SCALAR_SHARE_FIRST = 0.5
+SCALAR_SHARE = 0.75
 TOKENS = 110
 FIRST_TOKEN = {1: 0, 3: 1, 6: 10, 8: 46}
 EPS = 1e-5
@@ -59,9 +60,8 @@ def tile_apnb_pa_t_kernel(
         grouped_pool = ctx.enter_context(tc.tile_pool(name="grouped", bufs=3))
         kf_pool = ctx.enter_context(tc.tile_pool(name="kf", bufs=8))
         pool_pool = ctx.enter_context(tc.tile_pool(name="pooling", bufs=2))
-        acc_pool = ctx.enter_context(tc.psum_pool(name="acc", bufs=6))
-        lane_pool = ctx.enter_context(tc.psum_pool(name="lanes", bufs=2))
-        ctx.enter_context(tc.manual_schedule())
+        acc_pool = ctx.enter_context(tc.psum_pool(name="acc", bufs=7))
+        flip_pool = ctx.enter_context(tc.psum_pool(name="flip", bufs=1))
 
         w_words = keep.tile([P, PASSES, 2 * OUT_CHANNELS], U8, align_bytes=64)
         w_scales = keep.tile([P, PASSES, OUT_CHANNELS], U8, align_bytes=64)
@@ -119,11 +119,9 @@ def tile_apnb_pa_t_kernel(
 
         identity = keep.tile([P, P], F32)
         make_identity(nc, identity[:])
-        identity_bf = keep.tile([P, P], BF16)
-        make_identity(nc, identity_bf[:])
         rows_f32 = keep.tile([P, P], F32)
         nc.vector.tensor_copy(out=rows_f32[:], in_=rows_bf[:])
-        flipped = lane_pool.tile([P, P], F32, tag="lanes")
+        flipped = flip_pool.tile([P, P], F32)
         nc.tensor.transpose(flipped[:], rows_f32[:], identity[:])
         par = keep.tile([P, P], F32)
         nc.vector.tensor_copy(out=par[:], in_=flipped[:])
@@ -150,22 +148,11 @@ def tile_apnb_pa_t_kernel(
             first, width = N_TILES[n_tile]
             raw = raw_tiles[stripe][g]
             grouped = grouped_pool.tile([P, N_TILE, PACK], BF16, align_bytes=64)
-            if width == N_TILE:
-                for lo in range(0, width, LANE_COLS):
-                    lanes = lane_pool.tile([P, LANE_COLS, PACK], BF16, tag="lanes")
-                    for j in range(0, PACK, 2):
-                        nc.tensor.matmul(
-                            out=lanes[:, :, j : j + 2].rearrange("p c j -> p j c"),
-                            lhsT=identity_bf[:],
-                            rhs=raw[:, j : j + 2, first + lo : first + lo + LANE_COLS],
-                            start=True,
-                            stop=True,
-                        )
-                    nc.scalar.copy(out=grouped[:, lo : lo + LANE_COLS, :], in_=lanes[:])
-            else:
-                nc.vector.tensor_copy(
-                    out=grouped[:, 0:width, :].rearrange("p (c i) j -> p c j i", i=4),
-                    in_=raw[:, :, first : first + width].rearrange("p j (c i) -> p c j i", i=4),
+            split = int(width * (SCALAR_SHARE_FIRST if stripe == 0 else SCALAR_SHARE))
+            for copy, lo, hi in ((nc.scalar.copy, 0, split), (nc.vector.tensor_copy, split, width)):
+                copy(
+                    out=grouped[:, lo:hi, :].rearrange("p (c i) j -> p c j i", i=4),
+                    in_=raw[:, :, first + lo : first + hi].rearrange("p j (c i) -> p c j i", i=4),
                 )
             return grouped
 
@@ -260,7 +247,7 @@ def tile_apnb_pa_t_kernel(
                 out=out_1[image].rearrange("(m p) t -> p m t", p=P),
                 in_=tokens[:, image, 0:KEY_TILES, 0:TOKENS],
             )
-            flipped = lane_pool.tile([P, P], F32, tag="lanes")
+            flipped = flip_pool.tile([P, P], F32)
             nc.tensor.transpose(flipped[:], tokens[:, image, VALUE_TILE, :], identity[:])
             value = pool_pool.tile([P, P], F32)
             nc.scalar.copy(out=value[:], in_=flipped[:])

@@ -22,28 +22,23 @@ CHANNELS = 1024
 PASSES = CHANNELS // K_PASS
 SIDE = 48
 IMAGE_POS = SIDE * SIDE
-POSITIONS = IMAGES * IMAGE_POS
 KEY_TILES = 8
 VALUE_TILE = 8
 OUT_TILES = KEY_TILES + 1
 OUT_CHANNELS = OUT_TILES * P
-N_TILE = 512
-STRIPE_ROWS = 24
-STRIPE = STRIPE_ROWS * SIDE
-IMAGE_STRIPES = IMAGE_POS // STRIPE
-STRIPES = IMAGES * IMAGE_STRIPES
-N_TILES = ((0, N_TILE), (N_TILE, N_TILE), (2 * N_TILE, STRIPE - 2 * N_TILE))
-UNITS = len(N_TILES) * PASSES
-GROUP = 3
-STRIPE_GRID = STRIPE // 4
+BANK = 512
+NARROW = 128
+BANKS = ((0, 512), (512, 512), (1024, 512), (1536, 512), (2048, 256))
+PIECES = ((0, 1024), (1024, 1024), (2048, 256))
+UNITS = len(PIECES) * PASSES
+SCALAR_SHARE = 0.5
 HALF = SIDE // 2
-SCALAR_SHARE_FIRST = 0.5
-SCALAR_SHARE = 0.75
+GROUP = 3
 TOKENS = 110
 FIRST_TOKEN = {1: 0, 3: 1, 6: 10, 8: 46}
 EPS = 1e-5
 
-FLOPS = 2 * POSITIONS * CHANNELS * OUT_CHANNELS
+FLOPS = 2 * IMAGES * IMAGE_POS * CHANNELS * OUT_CHANNELS
 
 ROW_BK, ROW_GK, ROW_BETAK, ROW_MK, ROW_VK, ROW_BV = 0, 8, 16, 24, 32, 40
 
@@ -57,16 +52,17 @@ def tile_apnb_pa_t_kernel(
 
     with ExitStack() as ctx:
         keep = ctx.enter_context(tc.tile_pool(name="keep", bufs=1))
-        grouped_pool = ctx.enter_context(tc.tile_pool(name="grouped", bufs=3))
-        kf_pool = ctx.enter_context(tc.tile_pool(name="kf", bufs=8))
+        grouped_pool = ctx.enter_context(tc.tile_pool(name="grouped", bufs=2))
+        kf_pool = ctx.enter_context(tc.tile_pool(name="kf", bufs=4))
         pool_pool = ctx.enter_context(tc.tile_pool(name="pooling", bufs=2))
+        band_pool = ctx.enter_context(tc.tile_pool(name="bands", bufs=1))
         acc_pool = ctx.enter_context(tc.psum_pool(name="acc", bufs=7))
         flip_pool = ctx.enter_context(tc.psum_pool(name="flip", bufs=1))
 
         w_words = keep.tile([P, PASSES, 2 * OUT_CHANNELS], U8, align_bytes=64)
         w_scales = keep.tile([P, PASSES, OUT_CHANNELS], U8, align_bytes=64)
-        x_codes = keep.tile([P, PASSES, POSITIONS], U32, align_bytes=64)
-        x_scales = keep.tile([P, PASSES, POSITIONS], U8, align_bytes=64)
+        x_codes = keep.tile([P, IMAGES, PASSES, IMAGE_POS], U32, align_bytes=64)
+        x_scales = keep.tile([P, IMAGES, PASSES, IMAGE_POS], U8, align_bytes=64)
         sum8 = keep.tile([P, IMAGES, OUT_TILES, 64], F32)
         sum6 = keep.tile([P, IMAGES, OUT_TILES, 36], F32)
         sum3 = keep.tile([P, IMAGES, OUT_TILES, 9], F32)
@@ -75,15 +71,17 @@ def tile_apnb_pa_t_kernel(
         scale_all = keep.tile([P, OUT_TILES], F32)
         shift_all = keep.tile([P, OUT_TILES], F32)
 
-        def load_stripe(stripe):
-            image, part = divmod(stripe, IMAGE_STRIPES)
-            tiles = [keep.tile([P, PACK, STRIPE], BF16, name="raw%d_%d" % (stripe, g)) for g in range(PASSES)]
-            for first, width in N_TILES if stripe == 0 else ((0, STRIPE),):
-                for g in range(PASSES):
-                    nc.sync.dma_start(
-                        out=tiles[g][:, :, first : first + width],
-                        in_=feats_rows[image, g, :, :, part * STRIPE + first : part * STRIPE + first + width],
-                    )
+        def unit_of(step):
+            piece, g = divmod(step, PASSES)
+            return g, PIECES[piece][0], PIECES[piece][1]
+
+        def load_image(image):
+            tiles = []
+            for step in range(UNITS):
+                g, first, width = unit_of(step)
+                raw = keep.tile([P, PACK, width], BF16, name="raw%d_%d" % (image, step))
+                nc.sync.dma_start(out=raw[:], in_=feats_rows[image, g, :, :, first : first + width])
+                tiles.append(raw)
             return tiles
 
         def load_scales(scales, first, width):
@@ -108,14 +106,12 @@ def tile_apnb_pa_t_kernel(
             blocks = vector.rearrange("(m c) -> m c", c=P)
             nc.scalar.dma_start(out=rows_bf[row : row + blocks.shape[0], :], in_=blocks)
         nc.vector.memset(w_scales[:].rearrange("p g n -> p (g n)").bitcast(I32), 0)
-        raw_tiles = [load_stripe(0)]
+        raw_tiles = [load_image(0)]
         load_scales(Wk_scales, 0, KEY_TILES * P)
         load_words(Wk_words, 0, 2 * KEY_TILES * P)
         load_words(Wv_words, 2 * KEY_TILES * P, 2 * P)
-        raw_tiles.append(load_stripe(1))
         load_scales(Wv_scales, KEY_TILES * P, P)
-        raw_tiles.append(load_stripe(2))
-        raw_tiles.append(load_stripe(3))
+        raw_tiles.append(load_image(1))
 
         identity = keep.tile([P, P], F32)
         make_identity(nc, identity[:])
@@ -143,51 +139,47 @@ def tile_apnb_pa_t_kernel(
         nc.vector.tensor_copy(out=shift_all[:, VALUE_TILE : VALUE_TILE + 1], in_=par[:, ROW_BV : ROW_BV + 1])
         nc.vector.memset(tokens[:, :, VALUE_TILE, :], 0.0)
 
-        def regroup_unit(stripe, unit):
-            n_tile, g = divmod(unit, PASSES)
-            first, width = N_TILES[n_tile]
-            raw = raw_tiles[stripe][g]
-            grouped = grouped_pool.tile([P, N_TILE, PACK], BF16, align_bytes=64)
-            split = int(width * (SCALAR_SHARE_FIRST if stripe == 0 else SCALAR_SHARE))
+        def regroup_unit(image, step):
+            g, first, width = unit_of(step)
+            grouped = grouped_pool.tile([P, PIECES[0][1], PACK], BF16, align_bytes=64)
+            split = int(width * SCALAR_SHARE)
             for copy, lo, hi in ((nc.scalar.copy, 0, split), (nc.vector.tensor_copy, split, width)):
                 copy(
                     out=grouped[:, lo:hi, :].rearrange("p (c i) j -> p c j i", i=4),
-                    in_=raw[:, :, first + lo : first + hi].rearrange("p j (c i) -> p c j i", i=4),
+                    in_=raw_tiles[image][step][:, :, lo:hi].rearrange("p j (c i) -> p c j i", i=4),
                 )
             return grouped
 
-        def quantise_unit(stripe, unit, grouped):
-            n_tile, g = divmod(unit, PASSES)
-            first, width = N_TILES[n_tile]
-            cols = slice(stripe * STRIPE + first, stripe * STRIPE + first + width)
+        def quantise_unit(image, step, grouped):
+            g, first, width = unit_of(step)
             nc.vector.quantize_mx(
-                out=x_codes[:, g, cols].bitcast(FP8X4),
-                scales=x_scales[:, g, cols],
+                out=x_codes[:, image, g, first : first + width].bitcast(FP8X4),
+                scales=x_scales[:, image, g, first : first + width],
                 in_=grouped[:, 0:width, :].rearrange("p c j -> p (c j)"),
             )
 
-        def prepare_step(stripe, step, waiting):
+        def prepare_step(image, step, waiting):
             if step < UNITS:
-                waiting.append(regroup_unit(stripe, step))
+                waiting.append(regroup_unit(image, step))
             if 0 < step <= UNITS:
-                quantise_unit(stripe, step - 1, waiting[step - 1])
+                quantise_unit(image, step - 1, waiting[step - 1])
 
-        def project(stripe, m):
-            image, part = divmod(stripe, IMAGE_STRIPES)
-            kf = kf_pool.tile([P, STRIPE], F32)
-            for first, width in N_TILES:
-                cols = slice(stripe * STRIPE + first, stripe * STRIPE + first + width)
-                acc = acc_pool.tile([P, N_TILE], F32)
-                for g in range(PASSES):
-                    nc.tensor.matmul_mx(
-                        out=acc[:, 0:width],
-                        lhsT=w_words[:, g, 2 * P * m : 2 * P * (m + 1)].bitcast(FP4X4),
-                        lhsT_scale=w_scales[:, g, P * m : P * (m + 1)],
-                        rhs=x_codes[:, g, cols].bitcast(FP8X4),
-                        rhs_scale=x_scales[:, g, cols],
-                        start=(g == 0),
-                        stop=(g == PASSES - 1),
-                    )
+        def project(image, m):
+            kf = kf_pool.tile([P, IMAGE_POS], F32)
+            for first, width in BANKS:
+                acc = acc_pool.tile([P, BANK], F32)
+                n = BANK if width == BANK else NARROW
+                for lo in range(0, width, n):
+                    for g in range(PASSES):
+                        nc.tensor.matmul_mx(
+                            out=acc[:, lo : lo + n],
+                            lhsT=w_words[:, g, 2 * P * m : 2 * P * (m + 1)].bitcast(FP4X4),
+                            lhsT_scale=w_scales[:, g, P * m : P * (m + 1)],
+                            rhs=x_codes[:, image, g, first + lo : first + lo + n].bitcast(FP8X4),
+                            rhs_scale=x_scales[:, image, g, first + lo : first + lo + n],
+                            start=(g == 0),
+                            stop=(g == PASSES - 1),
+                        )
                 nc.scalar.activation(
                     out=kf[:, first : first + width],
                     in_=acc[:, 0:width],
@@ -196,34 +188,47 @@ def tile_apnb_pa_t_kernel(
                     scale=scale_all[:, m : m + 1],
                 )
             if m < KEY_TILES:
-                nc.sync.dma_start(
-                    out=kf_out[image, P * m : P * (m + 1), part * STRIPE : (part + 1) * STRIPE], in_=kf[:]
-                )
+                nc.sync.dma_start(out=kf_out[image, P * m : P * (m + 1), :], in_=kf[:])
             return kf
 
-        def add_row_pairs(kf, row_pairs, slot):
+        def add_squares(kf, squares, slot):
             rows = kf[:].rearrange("p (r two w) -> p r two w", two=2, w=SIDE)
+            row_pairs = pool_pool.tile([P, HALF, SIDE], F32)
+            nc.vector.tensor_tensor(out=row_pairs[:], in0=rows[:, :, 0, :], in1=rows[:, :, 1, :], op=ALU.add)
+            col_pairs = row_pairs[:].rearrange("p r (c two) -> p r c two", two=2)
             nc.vector.tensor_tensor(
-                out=row_pairs[:, slot, :].rearrange("p (r w) -> p r w", w=SIDE),
-                in0=rows[:, :, 0, :],
-                in1=rows[:, :, 1, :],
+                out=squares[:, slot * HALF : (slot + 1) * HALF, :],
+                in0=col_pairs[:, :, :, 0],
+                in1=col_pairs[:, :, :, 1],
                 op=ALU.add,
             )
 
-        def pool_group(stripe, m_first, row_pairs):
-            image, part = divmod(stripe, IMAGE_STRIPES)
-            col_pairs = row_pairs[:].rearrange("p m (c two) -> p (m c) two", two=2)
-            squares = pool_pool.tile([P, GROUP * STRIPE_GRID], F32)
-            nc.vector.tensor_tensor(out=squares[:], in0=col_pairs[:, :, 0], in1=col_pairs[:, :, 1], op=ALU.add)
-            for sums, cells in ((sum8, 8), (sum6, 6)):
-                side = HALF // cells
-                here = cells * cells // IMAGE_STRIPES
-                nc.vector.tensor_reduce(
-                    out=sums[:, image, m_first : m_first + GROUP, part * here : (part + 1) * here],
-                    in_=squares[:].rearrange("p (mb i bw j) -> p mb bw i j", i=side, bw=cells, j=side),
-                    axis=AXIS.XY,
-                    op=ALU.add,
-                )
+        def pool_fine_levels(image, m_first, squares):
+            rows = GROUP * HALF
+            by_two = squares[:].rearrange("p (r two) c -> p r two c", two=2)
+            two_rows = band_pool.tile([P, rows // 2, HALF], F32)
+            nc.vector.tensor_tensor(out=two_rows[:], in0=by_two[:, :, 0, :], in1=by_two[:, :, 1, :], op=ALU.add)
+            by_four = two_rows[:].rearrange("p (b two) c -> p b two c", two=2)
+            bands6 = band_pool.tile([P, rows // 4, HALF], F32)
+            nc.vector.tensor_tensor(out=bands6[:], in0=by_four[:, :, 0, :], in1=by_four[:, :, 1, :], op=ALU.add)
+            six_rows = squares[:].rearrange("p (s r) c -> p s r c", r=6)
+            three_pairs = two_rows[:].rearrange("p (s r) c -> p s r c", r=3)
+            bands8 = band_pool.tile([P, rows // 6, 2, HALF], F32)
+            nc.vector.tensor_tensor(
+                out=bands8[:], in0=three_pairs[:, :, 0:3:2, :], in1=six_rows[:, :, 2:4, :], op=ALU.add
+            )
+            nc.vector.tensor_reduce(
+                out=sum8[:, image, m_first : m_first + GROUP, :],
+                in_=bands8[:].rearrange("p s e (bw j) -> p (s e bw) j", j=3),
+                axis=AXIS.X,
+                op=ALU.add,
+            )
+            nc.vector.tensor_reduce(
+                out=sum6[:, image, m_first : m_first + GROUP, :],
+                in_=bands6[:].rearrange("p b (bw j) -> p (b bw) j", j=4),
+                axis=AXIS.X,
+                op=ALU.add,
+            )
 
         def sum_coarse_levels(image):
             nc.vector.tensor_reduce(
@@ -256,18 +261,17 @@ def tile_apnb_pa_t_kernel(
         waiting = []
         for step in range(UNITS + 1):
             prepare_step(0, step, waiting)
-        for stripe in range(STRIPES):
+        for image in range(IMAGES):
             waiting = []
             for m in range(OUT_TILES):
-                kf = project(stripe, m)
-                if stripe + 1 < STRIPES:
-                    prepare_step(stripe + 1, m, waiting)
+                kf = project(image, m)
+                if image + 1 < IMAGES:
+                    prepare_step(image + 1, m, waiting)
                 if m % GROUP == 0:
-                    row_pairs = pool_pool.tile([P, GROUP, STRIPE // 2], F32)
-                add_row_pairs(kf, row_pairs, m % GROUP)
+                    squares = pool_pool.tile([P, GROUP * HALF, HALF], F32)
+                add_squares(kf, squares, m % GROUP)
                 if m % GROUP == GROUP - 1:
-                    pool_group(stripe, m - GROUP + 1, row_pairs)
-            if stripe % IMAGE_STRIPES == IMAGE_STRIPES - 1:
-                sum_coarse_levels(stripe // IMAGE_STRIPES)
+                    pool_fine_levels(image, m - GROUP + 1, squares)
+            sum_coarse_levels(image)
         for image in range(IMAGES):
             store_tokens(image)

@@ -25,6 +25,9 @@ IMAGE_POS = SIDE * SIDE
 KEY_TILES = 8
 VALUE_TILE = 8
 OUT_TILES = KEY_TILES + 1
+TILE_ORDER = (VALUE_TILE,) + tuple(range(KEY_TILES))
+VALUE_SLOT = 0
+FIRST_KEY_SLOT = 1
 OUT_CHANNELS = OUT_TILES * P
 BANK = 512
 NARROW = 128
@@ -137,7 +140,7 @@ def tile_apnb_pa_t_kernel(
         nc.vector.tensor_add(out=key_shift, in0=key_shift, in1=par_cols(ROW_BETAK))
         nc.vector.memset(scale_all[:, VALUE_TILE : VALUE_TILE + 1], 1.0)
         nc.vector.tensor_copy(out=shift_all[:, VALUE_TILE : VALUE_TILE + 1], in_=par[:, ROW_BV : ROW_BV + 1])
-        nc.vector.memset(tokens[:, :, VALUE_TILE, :], 0.0)
+        nc.vector.memset(tokens[:, :, VALUE_SLOT, :], 0.0)
 
         def regroup_unit(image, step):
             g, first, width = unit_of(step)
@@ -230,48 +233,53 @@ def tile_apnb_pa_t_kernel(
                 op=ALU.add,
             )
 
-        def sum_coarse_levels(image):
+        def make_tokens(image, first, slots):
+            some = slice(first, first + slots)
             nc.vector.tensor_reduce(
-                out=sum3[:, image],
-                in_=sum6[:, image]
+                out=sum3[:, image, some],
+                in_=sum6[:, image, some]
                 .rearrange("p m c -> p (m c)")
                 .rearrange("p (mb i bw j) -> p mb bw i j", i=2, bw=3, j=2),
                 axis=AXIS.XY,
                 op=ALU.add,
             )
-            nc.vector.tensor_reduce(out=sum1[:, image], in_=sum3[:, image], axis=AXIS.X, op=ALU.add)
-
-        def store_tokens(image):
+            nc.vector.tensor_reduce(out=sum1[:, image, some], in_=sum3[:, image, some], axis=AXIS.X, op=ALU.add)
             for sums, cells in ((sum8, 8), (sum6, 6), (sum3, 3), (sum1, 1)):
                 nc.scalar.mul(
-                    out=tokens[:, image, :, FIRST_TOKEN[cells] : FIRST_TOKEN[cells] + cells * cells],
-                    in_=sums[:, image],
+                    out=tokens[:, image, some, FIRST_TOKEN[cells] : FIRST_TOKEN[cells] + cells * cells],
+                    in_=sums[:, image, some],
                     mul=float(cells * cells) / IMAGE_POS,
                 )
-            nc.sync.dma_start(
-                out=out_1[image].rearrange("(m p) t -> p m t", p=P),
-                in_=tokens[:, image, 0:KEY_TILES, 0:TOKENS],
-            )
+
+        def store_value(image):
+            make_tokens(image, VALUE_SLOT, 1)
             flipped = flip_pool.tile([P, P], F32)
-            nc.tensor.transpose(flipped[:], tokens[:, image, VALUE_TILE, :], identity[:])
+            nc.tensor.transpose(flipped[:], tokens[:, image, VALUE_SLOT, :], identity[:])
             value = pool_pool.tile([P, P], F32)
             nc.scalar.copy(out=value[:], in_=flipped[:])
             nc.sync.dma_start(out=out_2[image], in_=value[0:TOKENS, :])
+
+        def store_keys(image):
+            make_tokens(image, FIRST_KEY_SLOT, KEY_TILES)
+            nc.sync.dma_start(
+                out=out_1[image].rearrange("(m p) t -> p m t", p=P),
+                in_=tokens[:, image, FIRST_KEY_SLOT : FIRST_KEY_SLOT + KEY_TILES, 0:TOKENS],
+            )
 
         waiting = []
         for step in range(UNITS + 1):
             prepare_step(0, step, waiting)
         for image in range(IMAGES):
             waiting = []
-            for m in range(OUT_TILES):
+            for slot, m in enumerate(TILE_ORDER):
                 kf = project(image, m)
                 if image + 1 < IMAGES:
-                    prepare_step(image + 1, m, waiting)
-                if m % GROUP == 0:
+                    prepare_step(image + 1, slot, waiting)
+                if slot % GROUP == 0:
                     squares = pool_pool.tile([P, GROUP * HALF, HALF], F32)
-                add_squares(kf, squares, m % GROUP)
-                if m % GROUP == GROUP - 1:
-                    pool_fine_levels(image, m - GROUP + 1, squares)
-            sum_coarse_levels(image)
-        for image in range(IMAGES):
-            store_tokens(image)
+                add_squares(kf, squares, slot % GROUP)
+                if slot % GROUP == GROUP - 1:
+                    pool_fine_levels(image, slot - GROUP + 1, squares)
+                if slot == GROUP - 1:
+                    store_value(image)
+            store_keys(image)

@@ -252,18 +252,17 @@ def tile_apnb_pa_t_kernel(
                 )
 
         def store_value(image):
-            make_tokens(image, VALUE_SLOT, 1)
             flipped = flip_pool.tile([P, P], F32)
             nc.tensor.transpose(flipped[:], tokens[:, image, VALUE_SLOT, :], identity[:])
             value = pool_pool.tile([P, P], F32)
             nc.scalar.copy(out=value[:], in_=flipped[:])
             nc.sync.dma_start(out=out_2[image], in_=value[0:TOKENS, :])
 
-        def store_keys(image):
-            make_tokens(image, FIRST_KEY_SLOT, KEY_TILES)
+        def store_keys(image, first, slots):
+            m_first = TILE_ORDER[first]
             nc.sync.dma_start(
-                out=out_1[image].rearrange("(m p) t -> p m t", p=P),
-                in_=tokens[:, image, FIRST_KEY_SLOT : FIRST_KEY_SLOT + KEY_TILES, 0:TOKENS],
+                out=out_1[image, P * m_first : P * (m_first + slots), :].rearrange("(m p) t -> p m t", p=P),
+                in_=tokens[:, image, first : first + slots, 0:TOKENS],
             )
 
         waiting = []
@@ -279,7 +278,11 @@ def tile_apnb_pa_t_kernel(
                     squares = pool_pool.tile([P, GROUP * HALF, HALF], F32)
                 add_squares(kf, squares, slot % GROUP)
                 if slot % GROUP == GROUP - 1:
-                    pool_fine_levels(image, slot - GROUP + 1, squares)
-                if slot == GROUP - 1:
-                    store_value(image)
-            store_keys(image)
+                    group_first = slot - GROUP + 1
+                    pool_fine_levels(image, group_first, squares)
+                    make_tokens(image, group_first, GROUP)
+                    if group_first == VALUE_SLOT:
+                        store_value(image)
+                        store_keys(image, FIRST_KEY_SLOT, GROUP - 1)
+                    else:
+                        store_keys(image, group_first, GROUP)

@@ -37,6 +37,7 @@ UNITS = len(PIECES) * PASSES
 SCALAR_SHARE = 0.5
 HALF = SIDE // 2
 GROUP = 3
+GROUPS = ((GROUP, GROUP, GROUP), (GROUP, GROUP, 2, 1))
 TOKENS = 110
 FIRST_TOKEN = {1: 0, 3: 1, 6: 10, 8: 46}
 EPS = 1e-5
@@ -206,28 +207,29 @@ def tile_apnb_pa_t_kernel(
                 op=ALU.add,
             )
 
-        def pool_fine_levels(image, m_first, squares):
-            rows = GROUP * HALF
-            by_two = squares[:].rearrange("p (r two) c -> p r two c", two=2)
+        def pool_fine_levels(image, m_first, count, all_squares):
+            rows = count * HALF
+            squares = all_squares[:, 0:rows, :]
+            by_two = squares.rearrange("p (r two) c -> p r two c", two=2)
             two_rows = band_pool.tile([P, rows // 2, HALF], F32)
             nc.vector.tensor_tensor(out=two_rows[:], in0=by_two[:, :, 0, :], in1=by_two[:, :, 1, :], op=ALU.add)
             by_four = two_rows[:].rearrange("p (b two) c -> p b two c", two=2)
             bands6 = band_pool.tile([P, rows // 4, HALF], F32)
             nc.vector.tensor_tensor(out=bands6[:], in0=by_four[:, :, 0, :], in1=by_four[:, :, 1, :], op=ALU.add)
-            six_rows = squares[:].rearrange("p (s r) c -> p s r c", r=6)
+            six_rows = squares.rearrange("p (s r) c -> p s r c", r=6)
             three_pairs = two_rows[:].rearrange("p (s r) c -> p s r c", r=3)
             bands8 = band_pool.tile([P, rows // 6, 2, HALF], F32)
             nc.vector.tensor_tensor(
                 out=bands8[:], in0=three_pairs[:, :, 0:3:2, :], in1=six_rows[:, :, 2:4, :], op=ALU.add
             )
             nc.vector.tensor_reduce(
-                out=sum8[:, image, m_first : m_first + GROUP, :],
+                out=sum8[:, image, m_first : m_first + count, :],
                 in_=bands8[:].rearrange("p s e (bw j) -> p (s e bw) j", j=3),
                 axis=AXIS.X,
                 op=ALU.add,
             )
             nc.vector.tensor_reduce(
-                out=sum6[:, image, m_first : m_first + GROUP, :],
+                out=sum6[:, image, m_first : m_first + count, :],
                 in_=bands6[:].rearrange("p b (bw j) -> p (b bw) j", j=4),
                 axis=AXIS.X,
                 op=ALU.add,
@@ -270,19 +272,20 @@ def tile_apnb_pa_t_kernel(
             prepare_step(0, step, waiting)
         for image in range(IMAGES):
             waiting = []
-            for slot, m in enumerate(TILE_ORDER):
-                kf = project(image, m)
-                if image + 1 < IMAGES:
-                    prepare_step(image + 1, slot, waiting)
-                if slot % GROUP == 0:
-                    squares = pool_pool.tile([P, GROUP * HALF, HALF], F32)
-                add_squares(kf, squares, slot % GROUP)
-                if slot % GROUP == GROUP - 1:
-                    group_first = slot - GROUP + 1
-                    pool_fine_levels(image, group_first, squares)
-                    make_tokens(image, group_first, GROUP)
-                    if group_first == VALUE_SLOT:
-                        store_value(image)
-                        store_keys(image, FIRST_KEY_SLOT, GROUP - 1)
-                    else:
-                        store_keys(image, group_first, GROUP)
+            group_first = 0
+            for count in GROUPS[image]:
+                squares = pool_pool.tile([P, GROUP * HALF, HALF], F32)
+                for place in range(count):
+                    slot = group_first + place
+                    kf = project(image, TILE_ORDER[slot])
+                    if image + 1 < IMAGES:
+                        prepare_step(image + 1, slot, waiting)
+                    add_squares(kf, squares, place)
+                pool_fine_levels(image, group_first, count, squares)
+                make_tokens(image, group_first, count)
+                if group_first == VALUE_SLOT:
+                    store_value(image)
+                    store_keys(image, FIRST_KEY_SLOT, count - 1)
+                else:
+                    store_keys(image, group_first, count)
+                group_first += count

@@ -59,7 +59,7 @@ def tile_apnb_pa_t_kernel(
         grouped_pool = ctx.enter_context(tc.tile_pool(name="grouped", bufs=2))
         kf_pool = ctx.enter_context(tc.tile_pool(name="kf", bufs=4))
         pool_pool = ctx.enter_context(tc.tile_pool(name="pooling", bufs=2))
-        band_pool = ctx.enter_context(tc.tile_pool(name="bands", bufs=1))
+        band_pool = ctx.enter_context(tc.tile_pool(name="bands", bufs=2))
         acc_pool = ctx.enter_context(tc.psum_pool(name="acc", bufs=7))
         flip_pool = ctx.enter_context(tc.psum_pool(name="flip", bufs=1))
 

@@ -34,7 +34,7 @@ NARROW = 128
 BANKS = ((0, 512), (512, 512), (1024, 512), (1536, 512), (2048, 256))
 PIECES = ((0, 1024), (1024, 1024), (2048, 256))
 UNITS = len(PIECES) * PASSES
-SCALAR_SHARE = 0.5
+SCALAR_SHARE = 0.4375
 HALF = SIDE // 2
 GROUP = 3
 GROUPS = ((GROUP, GROUP, GROUP), (GROUP, GROUP, 2, 1))
@@ -146,8 +146,10 @@ def tile_apnb_pa_t_kernel(
         def regroup_unit(image, step):
             g, first, width = unit_of(step)
             grouped = grouped_pool.tile([P, PIECES[0][1], PACK], BF16, align_bytes=64)
-            split = int(width * SCALAR_SHARE)
+            split = int(width * SCALAR_SHARE) if width == PIECES[0][1] else width
             for copy, lo, hi in ((nc.scalar.copy, 0, split), (nc.vector.tensor_copy, split, width)):
+                if lo == hi:
+                    continue
                 copy(
                     out=grouped[:, lo:hi, :].rearrange("p (c i) j -> p c j i", i=4),
                     in_=raw_tiles[image][step][:, :, lo:hi].rearrange("p j (c i) -> p c j i", i=4),

from contextlib import ExitStack

import concourse.mybir as mybir
from concourse.masks import make_identity

F32 = mybir.dt.float32
BF16 = mybir.dt.bfloat16
U8 = mybir.dt.uint8
U32 = mybir.dt.uint32
I32 = mybir.dt.int32
FP8X4 = mybir.dt.float8_e4m3fn_x4
FP4X4 = mybir.dt.float4_e2m1fn_x4
ACT = mybir.ActivationFunctionType
ALU = mybir.AluOpType
AXIS = mybir.AxisListType

P = 128
PACK = 4
K_PASS = P * PACK
IMAGES = 2
CHANNELS = 1024
PASSES = CHANNELS // K_PASS
SIDE = 48
IMAGE_POS = SIDE * SIDE
KEY_TILES = 8
VALUE_TILE = 8
OUT_TILES = KEY_TILES + 1
TILE_ORDER = (VALUE_TILE,) + tuple(range(KEY_TILES))
VALUE_SLOT = 0
FIRST_KEY_SLOT = 1
OUT_CHANNELS = OUT_TILES * P
BANK = 512
NARROW = 128
BANKS = ((0, 512), (512, 512), (1024, 512), (1536, 512), (2048, 256))
PIECES = ((0, 1024), (1024, 1024), (2048, 256))
UNITS = len(PIECES) * PASSES
SCALAR_SHARE = 0.4375
HALF = SIDE // 2
GROUP = 3
GROUPS = ((GROUP, GROUP, GROUP), (GROUP, GROUP, 2, 1))
TOKENS = 110
FIRST_TOKEN = {1: 0, 3: 1, 6: 10, 8: 46}
EPS = 1e-5

FLOPS = 2 * IMAGES * IMAGE_POS * CHANNELS * OUT_CHANNELS

ROW_BK, ROW_GK, ROW_BETAK, ROW_MK, ROW_VK, ROW_BV = 0, 8, 16, 24, 32, 40


def tile_apnb_pa_t_kernel(
    tc, feats, Wk_words, Wk_scales, bk, gk, betak, mk, vk, Wv_words, Wv_scales, bv, out_0, out_1, out_2
):
    nc = tc.nc
    feats_rows = feats.rearrange("b (g p j) h w -> b g p j (h w)", g=PASSES, p=P, j=PACK)
    kf_out = out_0.rearrange("b c h w -> b c (h w)")

    with ExitStack() as ctx:
        keep = ctx.enter_context(tc.tile_pool(name="keep", bufs=1))
        grouped_pool = ctx.enter_context(tc.tile_pool(name="grouped", bufs=2))
        kf_pool = ctx.enter_context(tc.tile_pool(name="kf", bufs=4))
        pool_pool = ctx.enter_context(tc.tile_pool(name="pooling", bufs=2))
        band_pool = ctx.enter_context(tc.tile_pool(name="bands", bufs=2))
        acc_pool = ctx.enter_context(tc.psum_pool(name="acc", bufs=7))
        flip_pool = ctx.enter_context(tc.psum_pool(name="flip", bufs=1))

        w_words = keep.tile([P, PASSES, 2 * OUT_CHANNELS], U8, align_bytes=64)
        w_scales = keep.tile([P, PASSES, OUT_CHANNELS], U8, align_bytes=64)
        x_codes = keep.tile([P, IMAGES, PASSES, IMAGE_POS], U32, align_bytes=64)
        x_scales = keep.tile([P, IMAGES, PASSES, IMAGE_POS], U8, align_bytes=64)
        sum8 = keep.tile([P, IMAGES, OUT_TILES, 64], F32)
        sum6 = keep.tile([P, IMAGES, OUT_TILES, 36], F32)
        sum3 = keep.tile([P, IMAGES, OUT_TILES, 9], F32)
        sum1 = keep.tile([P, IMAGES, OUT_TILES, 1], F32)
        tokens = keep.tile([P, IMAGES, OUT_TILES, P], F32)
        scale_all = keep.tile([P, OUT_TILES], F32)
        shift_all = keep.tile([P, OUT_TILES], F32)

        def unit_of(step):
            piece, g = divmod(step, PASSES)
            return g, PIECES[piece][0], PIECES[piece][1]

        def load_image(image):
            tiles = []
            for step in range(UNITS):
                g, first, width = unit_of(step)
                raw = keep.tile([P, PACK, width], BF16, name="raw%d_%d" % (image, step))
                nc.sync.dma_start(out=raw[:], in_=feats_rows[image, g, :, :, first : first + width])
                tiles.append(raw)
            return tiles

        def load_scales(scales, first, width):
            for quadrant in range(4):
                nc.sync.dma_start(
                    out=w_scales[32 * quadrant : 32 * quadrant + 4, :, first : first + width].bitcast(I32),
                    in_=scales[:, 4 * quadrant : 4 * quadrant + 4, :].rearrange("g r n -> r g n").bitcast(I32),
                )

        def load_words(words, first, width):
            nc.sync.dma_start(
                out=w_words[:, :, first : first + width].bitcast(I32),
                in_=words.rearrange("g p n -> p g n").bitcast(I32),
            )

        warm = keep.tile([P, 1], F32)
        nc.vector.memset(warm[:], 1.0)
        nc.scalar.sqrt(out=warm[:], in_=warm[:])
        rows_bf = keep.tile([P, P], BF16)
        nc.vector.memset(rows_bf[:], 0.0)
        for vector, row in ((bk, ROW_BK), (gk, ROW_GK), (betak, ROW_BETAK), (mk, ROW_MK), (vk, ROW_VK), (bv, ROW_BV)):
            blocks = vector.rearrange("(m c) -> m c", c=P)
            nc.scalar.dma_start(out=rows_bf[row : row + blocks.shape[0], :], in_=blocks)
        nc.vector.memset(w_scales[:].rearrange("p g n -> p (g n)").bitcast(I32), 0)
        raw_tiles = [load_image(0)]
        load_scales(Wk_scales, 0, KEY_TILES * P)
        load_words(Wk_words, 0, 2 * KEY_TILES * P)
        load_words(Wv_words, 2 * KEY_TILES * P, 2 * P)
        load_scales(Wv_scales, KEY_TILES * P, P)
        raw_tiles.append(load_image(1))

        identity = keep.tile([P, P], F32)
        make_identity(nc, identity[:])
        rows_f32 = keep.tile([P, P], F32)
        nc.vector.tensor_copy(out=rows_f32[:], in_=rows_bf[:])
        flipped = flip_pool.tile([P, P], F32)
        nc.tensor.transpose(flipped[:], rows_f32[:], identity[:])
        par = keep.tile([P, P], F32)
        nc.vector.tensor_copy(out=par[:], in_=flipped[:])

        def par_cols(row):
            return par[:, row : row + KEY_TILES]

        key_scale = scale_all[:, 0:KEY_TILES]
        key_shift = shift_all[:, 0:KEY_TILES]
        spread = keep.tile([P, KEY_TILES], F32)
        nc.vector.tensor_scalar_add(out=spread[:], in0=par_cols(ROW_VK), scalar1=EPS)
        nc.scalar.sqrt(out=spread[:], in_=spread[:])
        nc.vector.reciprocal(out=spread[:], in_=spread[:])
        nc.vector.tensor_mul(out=key_scale, in0=par_cols(ROW_GK), in1=spread[:])
        nc.vector.tensor_sub(out=key_shift, in0=par_cols(ROW_BK), in1=par_cols(ROW_MK))
        nc.vector.tensor_mul(out=key_shift, in0=key_shift, in1=key_scale)
        nc.vector.tensor_add(out=key_shift, in0=key_shift, in1=par_cols(ROW_BETAK))
        nc.vector.memset(scale_all[:, VALUE_TILE : VALUE_TILE + 1], 1.0)
        nc.vector.tensor_copy(out=shift_all[:, VALUE_TILE : VALUE_TILE + 1], in_=par[:, ROW_BV : ROW_BV + 1])
        nc.vector.memset(tokens[:, :, VALUE_SLOT, :], 0.0)

        def regroup_unit(image, step):
            g, first, width = unit_of(step)
            grouped = grouped_pool.tile([P, PIECES[0][1], PACK], BF16, align_bytes=64)
            split = int(width * SCALAR_SHARE) if width == PIECES[0][1] else width
            for copy, lo, hi in ((nc.scalar.copy, 0, split), (nc.vector.tensor_copy, split, width)):
                if lo == hi:
                    continue
                copy(
                    out=grouped[:, lo:hi, :].rearrange("p (c i) j -> p c j i", i=4),
                    in_=raw_tiles[image][step][:, :, lo:hi].rearrange("p j (c i) -> p c j i", i=4),
                )
            return grouped

        def quantise_unit(image, step, grouped):
            g, first, width = unit_of(step)
            nc.vector.quantize_mx(
                out=x_codes[:, image, g, first : first + width].bitcast(FP8X4),
                scales=x_scales[:, image, g, first : first + width],
                in_=grouped[:, 0:width, :].rearrange("p c j -> p (c j)"),
            )

        def prepare_step(image, step, waiting):
            if step < UNITS:
                waiting.append(regroup_unit(image, step))
            if 0 < step <= UNITS:
                quantise_unit(image, step - 1, waiting[step - 1])

        def project(image, m):
            kf = kf_pool.tile([P, IMAGE_POS], F32)
            for first, width in BANKS:
                acc = acc_pool.tile([P, BANK], F32)
                n = BANK if width == BANK else NARROW
                for lo in range(0, width, n):
                    for g in range(PASSES):
                        nc.tensor.matmul_mx(
                            out=acc[:, lo : lo + n],
                            lhsT=w_words[:, g, 2 * P * m : 2 * P * (m + 1)].bitcast(FP4X4),
                            lhsT_scale=w_scales[:, g, P * m : P * (m + 1)],
                            rhs=x_codes[:, image, g, first + lo : first + lo + n].bitcast(FP8X4),
                            rhs_scale=x_scales[:, image, g, first + lo : first + lo + n],
                            start=(g == 0),
                            stop=(g == PASSES - 1),
                        )
                nc.scalar.activation(
                    out=kf[:, first : first + width],
                    in_=acc[:, 0:width],
                    func=ACT.Relu if m < KEY_TILES else ACT.Identity,
                    bias=shift_all[:, m : m + 1],
                    scale=scale_all[:, m : m + 1],
                )
            if m < KEY_TILES:
                nc.sync.dma_start(out=kf_out[image, P * m : P * (m + 1), :], in_=kf[:])
            return kf

        def add_squares(kf, squares, slot):
            rows = kf[:].rearrange("p (r two w) -> p r two w", two=2, w=SIDE)
            row_pairs = pool_pool.tile([P, HALF, SIDE], F32)
            nc.vector.tensor_tensor(out=row_pairs[:], in0=rows[:, :, 0, :], in1=rows[:, :, 1, :], op=ALU.add)
            col_pairs = row_pairs[:].rearrange("p r (c two) -> p r c two", two=2)
            nc.vector.tensor_tensor(
                out=squares[:, slot * HALF : (slot + 1) * HALF, :],
                in0=col_pairs[:, :, :, 0],
                in1=col_pairs[:, :, :, 1],
                op=ALU.add,
            )

        def pool_fine_levels(image, m_first, count, all_squares):
            rows = count * HALF
            squares = all_squares[:, 0:rows, :]
            by_two = squares.rearrange("p (r two) c -> p r two c", two=2)
            two_rows = band_pool.tile([P, rows // 2, HALF], F32)
            nc.vector.tensor_tensor(out=two_rows[:], in0=by_two[:, :, 0, :], in1=by_two[:, :, 1, :], op=ALU.add)
            by_four = two_rows[:].rearrange("p (b two) c -> p b two c", two=2)
            bands6 = band_pool.tile([P, rows // 4, HALF], F32)
            nc.vector.tensor_tensor(out=bands6[:], in0=by_four[:, :, 0, :], in1=by_four[:, :, 1, :], op=ALU.add)
            six_rows = squares.rearrange("p (s r) c -> p s r c", r=6)
            three_pairs = two_rows[:].rearrange("p (s r) c -> p s r c", r=3)
            bands8 = band_pool.tile([P, rows // 6, 2, HALF], F32)
            nc.vector.tensor_tensor(
                out=bands8[:], in0=three_pairs[:, :, 0:3:2, :], in1=six_rows[:, :, 2:4, :], op=ALU.add
            )
            nc.vector.tensor_reduce(
                out=sum8[:, image, m_first : m_first + count, :],
                in_=bands8[:].rearrange("p s e (bw j) -> p (s e bw) j", j=3),
                axis=AXIS.X,
                op=ALU.add,
            )
            nc.vector.tensor_reduce(
                out=sum6[:, image, m_first : m_first + count, :],
                in_=bands6[:].rearrange("p b (bw j) -> p (b bw) j", j=4),
                axis=AXIS.X,
                op=ALU.add,
            )

        def make_tokens(image, first, slots):
            some = slice(first, first + slots)
            nc.vector.tensor_reduce(
                out=sum3[:, image, some],
                in_=sum6[:, image, some]
                .rearrange("p m c -> p (m c)")
                .rearrange("p (mb i bw j) -> p mb bw i j", i=2, bw=3, j=2),
                axis=AXIS.XY,
                op=ALU.add,
            )
            nc.vector.tensor_reduce(out=sum1[:, image, some], in_=sum3[:, image, some], axis=AXIS.X, op=ALU.add)
            for sums, cells in ((sum8, 8), (sum6, 6), (sum3, 3), (sum1, 1)):
                nc.scalar.mul(
                    out=tokens[:, image, some, FIRST_TOKEN[cells] : FIRST_TOKEN[cells] + cells * cells],
                    in_=sums[:, image, some],
                    mul=float(cells * cells) / IMAGE_POS,
                )

        def store_value(image):
            flipped = flip_pool.tile([P, P], F32)
            nc.tensor.transpose(flipped[:], tokens[:, image, VALUE_SLOT, :], identity[:])
            value = pool_pool.tile([P, P], F32)
            nc.scalar.copy(out=value[:], in_=flipped[:])
            nc.sync.dma_start(out=out_2[image], in_=value[0:TOKENS, :])

        def store_keys(image, first, slots):
            m_first = TILE_ORDER[first]
            nc.sync.dma_start(
                out=out_1[image, P * m_first : P * (m_first + slots), :].rearrange("(m p) t -> p m t", p=P),
                in_=tokens[:, image, first : first + slots, 0:TOKENS],
            )

        waiting = []
        for step in range(UNITS + 1):
            prepare_step(0, step, waiting)
        for image in range(IMAGES):
            waiting = []
            group_first = 0
            for count in GROUPS[image]:
                squares = pool_pool.tile([P, GROUP * HALF, HALF], F32)
                for place in range(count):
                    slot = group_first + place
                    kf = project(image, TILE_ORDER[slot])
                    if image + 1 < IMAGES:
                        prepare_step(image + 1, slot, waiting)
                    add_squares(kf, squares, place)
                pool_fine_levels(image, group_first, count, squares)
                make_tokens(image, group_first, count)
                if group_first == VALUE_SLOT:
                    store_value(image)
                    store_keys(image, FIRST_KEY_SLOT, count - 1)
                else:
                    store_keys(image, group_first, count)
                group_first += count
